import numpy as np
import ml_dtypes


def mxq(x, axis, fmt="e4m3"):
    dtype, down = {"e4m3": (ml_dtypes.float8_e4m3fn, 7), "e5m2": (ml_dtypes.float8_e5m2, 14)}[fmt]
    v = np.moveaxis(np.asarray(x, np.float32).astype(ml_dtypes.bfloat16).astype(np.float64), axis, -1)
    blocks = v.reshape(v.shape[:-1] + (-1, 32))
    amax = np.abs(blocks).max(-1, keepdims=True)
    byte = np.maximum(np.where(amax > 0, np.frexp(amax)[1] - 1 + 127, 0) - down, 1)
    scale = np.exp2(byte - 127.0)
    codes = (blocks / scale).astype(np.float32).astype(dtype).astype(np.float64)
    return np.moveaxis((codes * scale).reshape(v.shape), -1, axis)


WIDE = False


def mx_kscale(k):
    if not WIDE:
        return np.ones(k)
    levels = np.array([10, -10, 5, -5, 0])
    a = np.random.permutation(np.resize(levels, k // 512 * 4)).reshape(k // 512, 4)
    idx = np.arange(k)
    return np.exp2(a[idx // 512, idx % 128 // 32])


BF16 = ml_dtypes.bfloat16


def bf(x):
    return np.asarray(x, np.float32).astype(BF16)


def f64(x):
    return np.asarray(x).astype(np.float64)


N_FFT, B, T = 1024, 16, 128
STRIDE = N_FFT + 1
L = T * STRIDE


def _fourier_kernels(n_fft):
    s = np.arange(n_fft, dtype=np.float64)
    k = np.arange(n_fft, dtype=np.float64)[:, None]
    ang = 2.0 * np.pi * k * s / n_fft
    return np.sin(ang), np.cos(ang)


def setup_inputs():
    s = mx_kscale(N_FFT)
    sx = np.concatenate([s, np.ones(1)])
    x = (np.random.standard_normal((1, B, T, STRIDE)) * sx).reshape(1, B, L)
    ws, wc = _fourier_kernels(N_FFT)
    wsin = (ws + 0.5 * np.random.standard_normal((N_FFT, N_FFT))) / np.sqrt(N_FFT) / s[None, :]
    wcos = (wc + 0.5 * np.random.standard_normal((N_FFT, N_FFT))) / np.sqrt(N_FFT) / s[None, :]
    return {"x": bf(x), "wsin": bf(wsin), "wcos": bf(wcos)}


def reference(x, wsin, wcos):
    sig = f64(x)[0]
    frames = sig.reshape(B, T, STRIDE)[..., :N_FFT]
    fq = mxq(frames, 2, "e4m3")
    real = np.einsum('btn,kn->tbk', fq, mxq(f64(wcos), 1, "e4m3"))
    imag = np.einsum('btn,kn->tbk', fq, mxq(f64(wsin), 1, "e4m3"))
    return real, -imag

@@ -1,0 +1,180 @@
+from contextlib import ExitStack
+
+import concourse.mybir as mybir
+from concourse.masks import make_identity
+
+BF16 = mybir.dt.bfloat16
+F32 = mybir.dt.float32
+U32 = mybir.dt.uint32
+U8 = mybir.dt.uint8
+FP8X4 = mybir.dt.float8_e4m3fn_x4
+
+P = 128
+N_FFT = 1024
+SIGNALS = 16
+FRAMES = 128
+STRIDE = N_FFT + 1
+PACK = 4
+K_PASS = P * PACK
+PASSES = N_FFT // K_PASS
+PLANES = 2
+WORDS = K_PASS // 2
+N_TILE = 512
+COL_TILES = N_FFT // N_TILE
+PAIR = 2
+ROUNDS = SIGNALS // PAIR
+W_CHUNKS = N_FFT // (PAIR * P)
+COS = 0
+SIN = 1
+
+FLOPS = 2 * 2 * SIGNALS * FRAMES * N_FFT * N_FFT
+
+
+def tile_dftlayer_kernel(tc, x, wsin, wcos, out_0, out_1):
+    nc = tc.nc
+    weights = {COS: wcos, SIN: wsin}
+    outputs = {COS: out_0, SIN: out_1}
+    signs = {COS: 1.0, SIN: -1.0}
+
+    with ExitStack() as ctx:
+        ctx.enter_context(tc.manual_schedule())
+        keep = ctx.enter_context(tc.tile_pool(name="keep", bufs=1))
+        stage = ctx.enter_context(tc.tile_pool(name="stage", bufs=4))
+        results = ctx.enter_context(tc.tile_pool(name="results", bufs=8))
+        psum_t = ctx.enter_context(tc.psum_pool(name="psum_t", bufs=4))
+        psum_acc = ctx.enter_context(tc.psum_pool(name="psum_acc", bufs=4))
+
+        ident = keep.tile([P, P], F32, name="ident")
+        make_identity(nc, ident[:])
+
+        x_frames = x.rearrange("o b (t s) -> t (o b) s", s=STRIDE)
+        x_raw = [keep.tile([P, PAIR, N_FFT], BF16, name="x_raw%d" % i) for i in range(ROUNDS)]
+        w_raw = {
+            (half, c): keep.tile([P, PAIR, N_FFT], BF16, name="w_raw%d_%d" % (half, c))
+            for half in (COS, SIN)
+            for c in range(W_CHUNKS)
+        }
+
+        def load_frames(i):
+            nc.sync.dma_start(out=x_raw[i][:], in_=x_frames[:, PAIR * i : PAIR * (i + 1), 0:N_FFT])
+
+        def load_weights(half):
+            rows = weights[half].rearrange("(c q r) n -> c q r n", q=P, r=PAIR)
+            for c in range(W_CHUNKS):
+                nc.sync.dma_start(out=w_raw[(half, c)][:], in_=rows[c, :, :, :])
+
+        load_frames(0)
+        load_weights(COS)
+        for i in range(1, ROUNDS):
+            load_frames(i)
+        load_weights(SIN)
+
+        def operand(name):
+            return {
+                "codes": keep.tile([P, N_TILE], U32, name=name + "_codes", align_bytes=64),
+                "scales": keep.tile([P, N_TILE], U8, name=name + "_scales", align_bytes=64),
+            }
+
+        frames_q = [operand("frames%d" % i) for i in range(ROUNDS)]
+        weights_q = {
+            (half, j, g): operand("w%d_%d_%d" % (half, j, g))
+            for half in (COS, SIN)
+            for j in range(COL_TILES)
+            for g in range(PASSES)
+        }
+
+        def transpose_bank(blocks):
+            bank = psum_t.tile([P, len(blocks), P], F32)
+            for s, block in enumerate(blocks):
+                nc.tensor.transpose(bank[:, s, :], block, ident[:])
+            return bank
+
+        def regroup_frames(i):
+            words = x_raw[i][:].bitcast(F32)
+            grouped = stage.tile([P, PAIR * N_FFT], BF16, align_bytes=64)
+            slots = grouped[:].bitcast(F32).rearrange(
+                "p (b g t u) -> p b g t u", b=PAIR, g=PASSES, u=PLANES
+            )
+            for b, copy in enumerate((nc.vector.tensor_copy, nc.scalar.copy)):
+                bank = transpose_bank(
+                    [words[:, b, P * s : P * (s + 1)] for s in range(PASSES * PLANES)]
+                )
+                copy(out=slots[:, b, :, :, :], in_=bank[:].rearrange("p (g u) t -> p g t u", u=PLANES))
+            return grouped, frames_q[i]
+
+        def regroup_weights(half, j, g):
+            grouped = stage.tile([P, PAIR * N_FFT], BF16, align_bytes=64)
+            slots = grouped[:].bitcast(F32).rearrange(
+                "p (c q r u) -> p c q r u", c=PAIR, r=PAIR, u=PLANES
+            )
+            for c, copy in enumerate((nc.vector.tensor_copy, nc.scalar.copy)):
+                words = w_raw[(half, PAIR * j + c)][:].bitcast(F32)
+                bank = transpose_bank(
+                    [
+                        words[:, r, WORDS * g + P * u : WORDS * g + P * (u + 1)]
+                        for r in range(PAIR)
+                        for u in range(PLANES)
+                    ]
+                )
+                copy(out=slots[:, c, :, :, :], in_=bank[:].rearrange("p (r u) q -> p q r u", u=PLANES))
+            return grouped, weights_q[(half, j, g)]
+
+        def quantise(job):
+            grouped, target = job
+            nc.vector.quantize_mx(
+                out=target["codes"][:].bitcast(FP8X4), scales=target["scales"][:], in_=grouped[:]
+            )
+
+        def transform(half, b, staged):
+            i, member = divmod(b, PAIR)
+            for j in range(COL_TILES):
+                acc = psum_acc.tile([P, N_TILE], F32)
+                for g in range(PASSES):
+                    first = (member * PASSES + g) * P
+                    nc.tensor.matmul_mx(
+                        out=acc[:],
+                        lhsT=frames_q[i]["codes"][:, first : first + P].bitcast(FP8X4),
+                        lhsT_scale=frames_q[i]["scales"][:, first : first + P],
+                        rhs=weights_q[(half, j, g)]["codes"][:].bitcast(FP8X4),
+                        rhs_scale=weights_q[(half, j, g)]["scales"][:],
+                        start=(g == 0),
+                        stop=(g == PASSES - 1),
+                    )
+                target = staged[:, member, N_TILE * j : N_TILE * (j + 1)]
+                if j % 2 == 0:
+                    nc.scalar.mul(out=target, in_=acc[:], mul=signs[half])
+                else:
+                    nc.vector.tensor_scalar_mul(out=target, in0=acc[:], scalar1=signs[half])
+
+        def store(half, i, staged):
+            nc.sync.dma_start(out=outputs[half][:, PAIR * i : PAIR * (i + 1), :], in_=staged[:])
+
+        waiting = regroup_frames(0)
+        for j in range(COL_TILES):
+            for g in range(PASSES):
+                regrouped = regroup_weights(COS, j, g)
+                quantise(waiting)
+                waiting = regrouped
+        quantise(waiting)
+
+        sin_units = [(j, g) for j in range(COL_TILES) for g in range(PASSES)]
+        first_sin_round = ROUNDS - len(sin_units)
+        for i in range(ROUNDS):
+            ahead = []
+            if i + 1 < ROUNDS:
+                ahead.append(regroup_frames(i + 1))
+            if i >= first_sin_round:
+                j, g = sin_units[i - first_sin_round]
+                ahead.append(regroup_weights(SIN, j, g))
+            staged = results.tile([P, PAIR, N_FFT], F32)
+            transform(COS, PAIR * i, staged)
+            for job in ahead:
+                quantise(job)
+            transform(COS, PAIR * i + 1, staged)
+            store(COS, i, staged)
+
+        for i in range(ROUNDS):
+            staged = results.tile([P, PAIR, N_FFT], F32)
+            for member in range(PAIR):
+                transform(SIN, PAIR * i + member, staged)
+            store(SIN, i, staged)

@@ -23,7 +23,8 @@ N_TILE = 512
 COL_TILES = N_FFT // N_TILE
 PAIR = 2
 ROUNDS = SIGNALS // PAIR
-W_CHUNKS = N_FFT // (PAIR * P)
+W_ROWS = PAIR * P
+W_CHUNKS = N_FFT // W_ROWS
 COS = 0
 SIN = 1
 
@@ -100,15 +101,18 @@ def tile_dftlayer_kernel(tc, x, wsin, wcos, out_0, out_1):
                     [words[:, b, P * s : P * (s + 1)] for s in range(PASSES * PLANES)]
                 )
                 copy(out=slots[:, b, :, :, :], in_=bank[:].rearrange("p (g u) t -> p g t u", u=PLANES))
-            return grouped, frames_q[i]
+            return [(grouped[:], frames_q[i]["codes"][:], frames_q[i]["scales"][:])]
 
-        def regroup_weights(half, j, g):
-            grouped = stage.tile([P, PAIR * N_FFT], BF16, align_bytes=64)
+        def regroup_weights(half, c):
+            words = w_raw[(half, c)][:].bitcast(F32)
+            grouped = stage.tile([P, PASSES * W_ROWS * PACK], BF16, align_bytes=64)
             slots = grouped[:].bitcast(F32).rearrange(
-                "p (c q r u) -> p c q r u", c=PAIR, r=PAIR, u=PLANES
+                "p (g q r u) -> p g q r u", g=PASSES, r=PAIR, u=PLANES
             )
-            for c, copy in enumerate((nc.vector.tensor_copy, nc.scalar.copy)):
-                words = w_raw[(half, PAIR * j + c)][:].bitcast(F32)
+            j, part = divmod(c, N_TILE // W_ROWS)
+            columns = slice(W_ROWS * part, W_ROWS * (part + 1))
+            jobs = []
+            for g, copy in enumerate((nc.vector.tensor_copy, nc.scalar.copy)):
                 bank = transpose_bank(
                     [
                         words[:, r, WORDS * g + P * u : WORDS * g + P * (u + 1)]
@@ -116,65 +120,73 @@ def tile_dftlayer_kernel(tc, x, wsin, wcos, out_0, out_1):
                         for u in range(PLANES)
                     ]
                 )
-                copy(out=slots[:, c, :, :, :], in_=bank[:].rearrange("p (r u) q -> p q r u", u=PLANES))
-            return grouped, weights_q[(half, j, g)]
+                copy(out=slots[:, g, :, :, :], in_=bank[:].rearrange("p (r u) q -> p q r u", u=PLANES))
+                jobs.append(
+                    (
+                        grouped[:, W_ROWS * PACK * g : W_ROWS * PACK * (g + 1)],
+                        weights_q[(half, j, g)]["codes"][:, columns],
+                        weights_q[(half, j, g)]["scales"][:, columns],
+                    )
+                )
+            return jobs
 
-        def quantise(job):
-            grouped, target = job
-            nc.vector.quantize_mx(
-                out=target["codes"][:].bitcast(FP8X4), scales=target["scales"][:], in_=grouped[:]
+        def quantise(jobs):
+            for values, codes, scales in jobs:
+                nc.vector.quantize_mx(out=codes.bitcast(FP8X4), scales=scales, in_=values)
+
+        def product(half, i, member, j, staged, turn):
+            acc = psum_acc.tile([P, N_TILE], F32)
+            for g in range(PASSES):
+                first = (member * PASSES + g) * P
+                nc.tensor.matmul_mx(
+                    out=acc[:],
+                    lhsT=frames_q[i]["codes"][:, first : first + P].bitcast(FP8X4),
+                    lhsT_scale=frames_q[i]["scales"][:, first : first + P],
+                    rhs=weights_q[(half, j, g)]["codes"][:].bitcast(FP8X4),
+                    rhs_scale=weights_q[(half, j, g)]["scales"][:],
+                    start=(g == 0),
+                    stop=(g == PASSES - 1),
+                )
+            target = staged[:, member, N_TILE * j : N_TILE * (j + 1)]
+            if turn == 0:
+                nc.scalar.mul(out=target, in_=acc[:], mul=signs[half])
+            else:
+                nc.vector.tensor_scalar_mul(out=target, in0=acc[:], scalar1=signs[half])
+
+        def store(half, i, staged, member, count):
+            first = PAIR * i + member
+            nc.sync.dma_start(
+                out=outputs[half][:, first : first + count, :],
+                in_=staged[:, member : member + count, :],
             )
 
-        def transform(half, b, staged):
-            i, member = divmod(b, PAIR)
-            for j in range(COL_TILES):
-                acc = psum_acc.tile([P, N_TILE], F32)
-                for g in range(PASSES):
-                    first = (member * PASSES + g) * P
-                    nc.tensor.matmul_mx(
-                        out=acc[:],
-                        lhsT=frames_q[i]["codes"][:, first : first + P].bitcast(FP8X4),
-                        lhsT_scale=frames_q[i]["scales"][:, first : first + P],
-                        rhs=weights_q[(half, j, g)]["codes"][:].bitcast(FP8X4),
-                        rhs_scale=weights_q[(half, j, g)]["scales"][:],
-                        start=(g == 0),
-                        stop=(g == PASSES - 1),
-                    )
-                target = staged[:, member, N_TILE * j : N_TILE * (j + 1)]
-                if j % 2 == 0:
-                    nc.scalar.mul(out=target, in_=acc[:], mul=signs[half])
-                else:
-                    nc.vector.tensor_scalar_mul(out=target, in0=acc[:], scalar1=signs[half])
-
-        def store(half, i, staged):
-            nc.sync.dma_start(out=outputs[half][:, PAIR * i : PAIR * (i + 1), :], in_=staged[:])
-
         waiting = regroup_frames(0)
-        for j in range(COL_TILES):
-            for g in range(PASSES):
-                regrouped = regroup_weights(COS, j, g)
-                quantise(waiting)
-                waiting = regrouped
+        for c in range(W_CHUNKS):
+            regrouped = regroup_weights(COS, c)
+            quantise(waiting)
+            waiting = regrouped
         quantise(waiting)
 
-        sin_units = [(j, g) for j in range(COL_TILES) for g in range(PASSES)]
-        first_sin_round = ROUNDS - len(sin_units)
         for i in range(ROUNDS):
             ahead = []
             if i + 1 < ROUNDS:
-                ahead.append(regroup_frames(i + 1))
-            if i >= first_sin_round:
-                j, g = sin_units[i - first_sin_round]
-                ahead.append(regroup_weights(SIN, j, g))
+                ahead += regroup_frames(i + 1)
+            if i >= ROUNDS - W_CHUNKS:
+                ahead += regroup_weights(SIN, i - (ROUNDS - W_CHUNKS))
             staged = results.tile([P, PAIR, N_FFT], F32)
-            transform(COS, PAIR * i, staged)
-            for job in ahead:
-                quantise(job)
-            transform(COS, PAIR * i + 1, staged)
-            store(COS, i, staged)
+            for j in range(COL_TILES):
+                for member in range(PAIR):
+                    product(COS, i, member, j, staged, turn=member)
+                if j == 0:
+                    quantise(ahead)
+            store(COS, i, staged, 0, PAIR)
 
         for i in range(ROUNDS):
             staged = results.tile([P, PAIR, N_FFT], F32)
             for member in range(PAIR):
-                transform(SIN, PAIR * i + member, staged)
-            store(SIN, i, staged)
+                for j in range(COL_TILES):
+                    product(SIN, i, member, j, staged, turn=j)
+                if i == ROUNDS - 1:
+                    store(SIN, i, staged, member, 1)
+            if i < ROUNDS - 1:
+                store(SIN, i, staged, 0, PAIR)

@@ -38,7 +38,6 @@ def tile_dftlayer_kernel(tc, x, wsin, wcos, out_0, out_1):
     signs = {COS: 1.0, SIN: -1.0}
 
     with ExitStack() as ctx:
-        ctx.enter_context(tc.manual_schedule())
         keep = ctx.enter_context(tc.tile_pool(name="keep", bufs=1))
         stage = ctx.enter_context(tc.tile_pool(name="stage", bufs=4))
         results = ctx.enter_context(tc.tile_pool(name="results", bufs=8))

from contextlib import ExitStack

import concourse.mybir as mybir
from concourse.masks import make_identity

BF16 = mybir.dt.bfloat16
F32 = mybir.dt.float32
U32 = mybir.dt.uint32
U8 = mybir.dt.uint8
FP8X4 = mybir.dt.float8_e4m3fn_x4

P = 128
N_FFT = 1024
SIGNALS = 16
FRAMES = 128
STRIDE = N_FFT + 1
PACK = 4
K_PASS = P * PACK
PASSES = N_FFT // K_PASS
PLANES = 2
WORDS = K_PASS // 2
N_TILE = 512
COL_TILES = N_FFT // N_TILE
PAIR = 2
ROUNDS = SIGNALS // PAIR
W_ROWS = PAIR * P
W_CHUNKS = N_FFT // W_ROWS
COS = 0
SIN = 1

FLOPS = 2 * 2 * SIGNALS * FRAMES * N_FFT * N_FFT


def tile_dftlayer_kernel(tc, x, wsin, wcos, out_0, out_1):
    nc = tc.nc
    weights = {COS: wcos, SIN: wsin}
    outputs = {COS: out_0, SIN: out_1}
    signs = {COS: 1.0, SIN: -1.0}

    with ExitStack() as ctx:
        keep = ctx.enter_context(tc.tile_pool(name="keep", bufs=1))
        stage = ctx.enter_context(tc.tile_pool(name="stage", bufs=4))
        results = ctx.enter_context(tc.tile_pool(name="results", bufs=8))
        psum_t = ctx.enter_context(tc.psum_pool(name="psum_t", bufs=4))
        psum_acc = ctx.enter_context(tc.psum_pool(name="psum_acc", bufs=4))

        ident = keep.tile([P, P], F32, name="ident")
        make_identity(nc, ident[:])

        x_frames = x.rearrange("o b (t s) -> t (o b) s", s=STRIDE)
        x_raw = [keep.tile([P, PAIR, N_FFT], BF16, name="x_raw%d" % i) for i in range(ROUNDS)]
        w_raw = {
            (half, c): keep.tile([P, PAIR, N_FFT], BF16, name="w_raw%d_%d" % (half, c))
            for half in (COS, SIN)
            for c in range(W_CHUNKS)
        }

        def load_frames(i):
            nc.sync.dma_start(out=x_raw[i][:], in_=x_frames[:, PAIR * i : PAIR * (i + 1), 0:N_FFT])

        def load_weights(half):
            rows = weights[half].rearrange("(c q r) n -> c q r n", q=P, r=PAIR)
            for c in range(W_CHUNKS):
                nc.sync.dma_start(out=w_raw[(half, c)][:], in_=rows[c, :, :, :])

        load_frames(0)
        load_weights(COS)
        for i in range(1, ROUNDS):
            load_frames(i)
        load_weights(SIN)

        def operand(name):
            return {
                "codes": keep.tile([P, N_TILE], U32, name=name + "_codes", align_bytes=64),
                "scales": keep.tile([P, N_TILE], U8, name=name + "_scales", align_bytes=64),
            }

        frames_q = [operand("frames%d" % i) for i in range(ROUNDS)]
        weights_q = {
            (half, j, g): operand("w%d_%d_%d" % (half, j, g))
            for half in (COS, SIN)
            for j in range(COL_TILES)
            for g in range(PASSES)
        }

        def transpose_bank(blocks):
            bank = psum_t.tile([P, len(blocks), P], F32)
            for s, block in enumerate(blocks):
                nc.tensor.transpose(bank[:, s, :], block, ident[:])
            return bank

        def regroup_frames(i):
            words = x_raw[i][:].bitcast(F32)
            grouped = stage.tile([P, PAIR * N_FFT], BF16, align_bytes=64)
            slots = grouped[:].bitcast(F32).rearrange(
                "p (b g t u) -> p b g t u", b=PAIR, g=PASSES, u=PLANES
            )
            for b, copy in enumerate((nc.vector.tensor_copy, nc.scalar.copy)):
                bank = transpose_bank(
                    [words[:, b, P * s : P * (s + 1)] for s in range(PASSES * PLANES)]
                )
                copy(out=slots[:, b, :, :, :], in_=bank[:].rearrange("p (g u) t -> p g t u", u=PLANES))
            return [(grouped[:], frames_q[i]["codes"][:], frames_q[i]["scales"][:])]

        def regroup_weights(half, c):
            words = w_raw[(half, c)][:].bitcast(F32)
            grouped = stage.tile([P, PASSES * W_ROWS * PACK], BF16, align_bytes=64)
            slots = grouped[:].bitcast(F32).rearrange(
                "p (g q r u) -> p g q r u", g=PASSES, r=PAIR, u=PLANES
            )
            j, part = divmod(c, N_TILE // W_ROWS)
            columns = slice(W_ROWS * part, W_ROWS * (part + 1))
            jobs = []
            for g, copy in enumerate((nc.vector.tensor_copy, nc.scalar.copy)):
                bank = transpose_bank(
                    [
                        words[:, r, WORDS * g + P * u : WORDS * g + P * (u + 1)]
                        for r in range(PAIR)
                        for u in range(PLANES)
                    ]
                )
                copy(out=slots[:, g, :, :, :], in_=bank[:].rearrange("p (r u) q -> p q r u", u=PLANES))
                jobs.append(
                    (
                        grouped[:, W_ROWS * PACK * g : W_ROWS * PACK * (g + 1)],
                        weights_q[(half, j, g)]["codes"][:, columns],
                        weights_q[(half, j, g)]["scales"][:, columns],
                    )
                )
            return jobs

        def quantise(jobs):
            for values, codes, scales in jobs:
                nc.vector.quantize_mx(out=codes.bitcast(FP8X4), scales=scales, in_=values)

        def product(half, i, member, j, staged, turn):
            acc = psum_acc.tile([P, N_TILE], F32)
            for g in range(PASSES):
                first = (member * PASSES + g) * P
                nc.tensor.matmul_mx(
                    out=acc[:],
                    lhsT=frames_q[i]["codes"][:, first : first + P].bitcast(FP8X4),
                    lhsT_scale=frames_q[i]["scales"][:, first : first + P],
                    rhs=weights_q[(half, j, g)]["codes"][:].bitcast(FP8X4),
                    rhs_scale=weights_q[(half, j, g)]["scales"][:],
                    start=(g == 0),
                    stop=(g == PASSES - 1),
                )
            target = staged[:, member, N_TILE * j : N_TILE * (j + 1)]
            if turn == 0:
                nc.scalar.mul(out=target, in_=acc[:], mul=signs[half])
            else:
                nc.vector.tensor_scalar_mul(out=target, in0=acc[:], scalar1=signs[half])

        def store(half, i, staged, member, count):
            first = PAIR * i + member
            nc.sync.dma_start(
                out=outputs[half][:, first : first + count, :],
                in_=staged[:, member : member + count, :],
            )

        waiting = regroup_frames(0)
        for c in range(W_CHUNKS):
            regrouped = regroup_weights(COS, c)
            quantise(waiting)
            waiting = regrouped
        quantise(waiting)

        for i in range(ROUNDS):
            ahead = []
            if i + 1 < ROUNDS:
                ahead += regroup_frames(i + 1)
            if i >= ROUNDS - W_CHUNKS:
                ahead += regroup_weights(SIN, i - (ROUNDS - W_CHUNKS))
            staged = results.tile([P, PAIR, N_FFT], F32)
            for j in range(COL_TILES):
                for member in range(PAIR):
                    product(COS, i, member, j, staged, turn=member)
                if j == 0:
                    quantise(ahead)
            store(COS, i, staged, 0, PAIR)

        for i in range(ROUNDS):
            staged = results.tile([P, PAIR, N_FFT], F32)
            for member in range(PAIR):
                for j in range(COL_TILES):
                    product(SIN, i, member, j, staged, turn=j)
                if i == ROUNDS - 1:
                    store(SIN, i, staged, member, 1)
            if i < ROUNDS - 1:
                store(SIN, i, staged, 0, PAIR)
